import numpy as np
import ml_dtypes

BF16 = ml_dtypes.bfloat16


def bf(x):
    return np.asarray(x, np.float32).astype(BF16)


def f32(x):
    return np.asarray(x, np.float32)


def f64(x):
    return np.asarray(x).astype(np.float64)


def striped(idx):
    return np.tile(idx.reshape(-1, 16).T, (8, 1))


C, S, N = 512, 2048, 512


def setup_inputs():
    return {"base": f32(np.random.standard_normal((C, S))), "tok0": f32(0.5 * np.random.standard_normal((C, N))), "tok1": f32(0.5 * np.random.standard_normal((C, N))), "tok2": f32(0.5 * np.random.standard_normal((C, N))), "tok3": f32(0.5 * np.random.standard_normal((C, N))), "offs": striped(np.random.permutation(S)[:N])}


def reference(base, tok0, tok1, tok2, tok3, offs):
    idx = offs[:16].T.reshape(-1)
    res = f64(base).copy()
    res[:, idx] = (f64(tok0) + f64(tok1)) + (f64(tok2) + f64(tok3))
    return res

@@ -1,0 +1,42 @@
+import concourse.mybir as mybir
+
+P = 128
+C, S, N = 512, 2048, 512
+BLOCKS = C // P
+F32 = mybir.dt.float32
+U16 = mybir.dt.uint16
+ADD = mybir.AluOpType.add
+
+BYTES = 4 * (C * S + 4 * C * N + C * (S - N)) + 2 * P * (N // 16)
+
+
+def tile_decoderrkbmemnn_s_kernel(tc, base, tok0, tok1, tok2, tok3, offs, out):
+    nc = tc.nc
+    with (
+        tc.tile_pool(name="held", bufs=1) as held,
+        tc.tile_pool(name="blocks", bufs=BLOCKS) as blocks,
+    ):
+        offsets = held.tile([P, N // 16], U16, name="offsets")
+        nc.sync.dma_start(offsets[:], offs)
+
+        for h in range(BLOCKS):
+            rows = slice(h * P, (h + 1) * P)
+
+            word0 = blocks.tile([P, N], F32, name="word0")
+            word1 = blocks.tile([P, N], F32, name="word1")
+            word2 = blocks.tile([P, N], F32, name="word2")
+            word3 = blocks.tile([P, N], F32, name="word3")
+            memory = blocks.tile([P, S], F32, name="memory")
+            nc.sync.dma_start(word0[:], tok0[rows, :])
+            nc.sync.dma_start(word1[:], tok1[rows, :])
+            nc.sync.dma_start(word2[:], tok2[rows, :])
+            nc.sync.dma_start(word3[:], tok3[rows, :])
+            nc.sync.dma_start(memory[:], base[rows, :])
+
+            pair01 = blocks.tile([P, N], F32, name="pair01")
+            pair23 = blocks.tile([P, N], F32, name="pair23")
+            nc.vector.tensor_tensor(pair01[:], word0[:], word1[:], ADD)
+            nc.vector.tensor_tensor(pair23[:], word2[:], word3[:], ADD)
+            nc.vector.tensor_tensor(memory[:].indirect(offsets[:]), pair01[:], pair23[:], ADD)
+
+            nc.scalar.dma_start(out[rows, :], memory[:])

@@ -12,31 +12,27 @@ BYTES = 4 * (C * S + 4 * C * N + C * (S - N)) + 2 * P * (N // 16)
 
 def tile_decoderrkbmemnn_s_kernel(tc, base, tok0, tok1, tok2, tok3, offs, out):
     nc = tc.nc
-    with (
-        tc.tile_pool(name="held", bufs=1) as held,
-        tc.tile_pool(name="blocks", bufs=BLOCKS) as blocks,
-    ):
+    toks = (tok0, tok1, tok2, tok3)
+    with tc.tile_pool(name="held", bufs=1) as held:
         offsets = held.tile([P, N // 16], U16, name="offsets")
         nc.sync.dma_start(offsets[:], offs)
 
+        words = []
+        memory = []
         for h in range(BLOCKS):
             rows = slice(h * P, (h + 1) * P)
+            words.append([held.tile([P, N], F32, name=f"word{w}_{h}") for w in range(4)])
+            memory.append(held.tile([P, S], F32, name=f"memory{h}"))
+            for w in range(4):
+                nc.sync.dma_start(words[h][w][:], toks[w][rows, :])
+            nc.sync.dma_start(memory[h][:], base[rows, :])
 
-            word0 = blocks.tile([P, N], F32, name="word0")
-            word1 = blocks.tile([P, N], F32, name="word1")
-            word2 = blocks.tile([P, N], F32, name="word2")
-            word3 = blocks.tile([P, N], F32, name="word3")
-            memory = blocks.tile([P, S], F32, name="memory")
-            nc.sync.dma_start(word0[:], tok0[rows, :])
-            nc.sync.dma_start(word1[:], tok1[rows, :])
-            nc.sync.dma_start(word2[:], tok2[rows, :])
-            nc.sync.dma_start(word3[:], tok3[rows, :])
-            nc.sync.dma_start(memory[:], base[rows, :])
+        for h in range(BLOCKS):
+            pair01 = held.tile([P, N], F32, name=f"pair01_{h}")
+            pair23 = held.tile([P, N], F32, name=f"pair23_{h}")
+            nc.vector.tensor_tensor(pair01[:], words[h][0][:], words[h][1][:], ADD)
+            nc.vector.tensor_tensor(pair23[:], words[h][2][:], words[h][3][:], ADD)
+            nc.vector.tensor_tensor(memory[h][:].indirect(offsets[:]), pair01[:], pair23[:], ADD)
 
-            pair01 = blocks.tile([P, N], F32, name="pair01")
-            pair23 = blocks.tile([P, N], F32, name="pair23")
-            nc.vector.tensor_tensor(pair01[:], word0[:], word1[:], ADD)
-            nc.vector.tensor_tensor(pair23[:], word2[:], word3[:], ADD)
-            nc.vector.tensor_tensor(memory[:].indirect(offsets[:]), pair01[:], pair23[:], ADD)
-
-            nc.scalar.dma_start(out[rows, :], memory[:])
+        for h in range(BLOCKS):
+            nc.sync.dma_start(out[h * P : (h + 1) * P, :], memory[h][:])

@@ -9,30 +9,41 @@ ADD = mybir.AluOpType.add
 
 BYTES = 4 * (C * S + 4 * C * N + C * (S - N)) + 2 * P * (N // 16)
 
+GROUP = 2
+GROUPS = BLOCKS // GROUP
+
 
 def tile_decoderrkbmemnn_s_kernel(tc, base, tok0, tok1, tok2, tok3, offs, out):
     nc = tc.nc
-    toks = (tok0, tok1, tok2, tok3)
+    toks = [tok.rearrange("(p h) n -> p (h n)", h=BLOCKS) for tok in (tok0, tok1, tok2, tok3)]
+    base_blocks = base.rearrange("(p h) s -> h p s", h=BLOCKS)
+    out_blocks = out.rearrange("(p h) s -> h p s", h=BLOCKS)
+
     with tc.tile_pool(name="held", bufs=1) as held:
         offsets = held.tile([P, N // 16], U16, name="offsets")
         nc.sync.dma_start(offsets[:], offs)
 
         words = []
         memory = []
-        for h in range(BLOCKS):
-            rows = slice(h * P, (h + 1) * P)
-            words.append([held.tile([P, N], F32, name=f"word{w}_{h}") for w in range(4)])
-            memory.append(held.tile([P, S], F32, name=f"memory{h}"))
+        for g in range(GROUPS):
+            columns = slice(g * GROUP * N, (g + 1) * GROUP * N)
+            words.append([held.tile([P, GROUP * N], F32, name=f"word{w}_{g}") for w in range(4)])
             for w in range(4):
-                nc.sync.dma_start(words[h][w][:], toks[w][rows, :])
-            nc.sync.dma_start(memory[h][:], base[rows, :])
+                nc.sync.dma_start(words[g][w][:], toks[w][:, columns])
+            for h in range(g * GROUP, (g + 1) * GROUP):
+                memory.append(held.tile([P, S], F32, name=f"memory{h}"))
+                nc.sync.dma_start(memory[h][:], base_blocks[h])
+
+        for g in range(GROUPS):
+            pair01 = held.tile([P, GROUP * N], F32, name=f"pair01_{g}")
+            pair23 = held.tile([P, GROUP * N], F32, name=f"pair23_{g}")
+            nc.vector.tensor_tensor(pair01[:], words[g][0][:], words[g][1][:], ADD)
+            nc.vector.tensor_tensor(pair23[:], words[g][2][:], words[g][3][:], ADD)
+            for i in range(GROUP):
+                entries = slice(i * N, (i + 1) * N)
+                nc.vector.tensor_tensor(
+                    memory[g * GROUP + i][:].indirect(offsets[:]), pair01[:, entries], pair23[:, entries], ADD
+                )
 
         for h in range(BLOCKS):
-            pair01 = held.tile([P, N], F32, name=f"pair01_{h}")
-            pair23 = held.tile([P, N], F32, name=f"pair23_{h}")
-            nc.vector.tensor_tensor(pair01[:], words[h][0][:], words[h][1][:], ADD)
-            nc.vector.tensor_tensor(pair23[:], words[h][2][:], words[h][3][:], ADD)
-            nc.vector.tensor_tensor(memory[h][:].indirect(offsets[:]), pair01[:], pair23[:], ADD)
-
-        for h in range(BLOCKS):
-            nc.sync.dma_start(out[h * P : (h + 1) * P, :], memory[h][:])
+            nc.sync.dma_start(out_blocks[h], memory[h][:])

@@ -21,7 +21,6 @@ def tile_decoderrkbmemnn_s_kernel(tc, base, tok0, tok1, tok2, tok3, offs, out):
 
     with tc.tile_pool(name="held", bufs=1) as held:
         offsets = held.tile([P, N // 16], U16, name="offsets")
-        nc.sync.dma_start(offsets[:], offs)
 
         words = []
         memory = []
@@ -30,6 +29,8 @@ def tile_decoderrkbmemnn_s_kernel(tc, base, tok0, tok1, tok2, tok3, offs, out):
             words.append([held.tile([P, GROUP * N], F32, name=f"word{w}_{g}") for w in range(4)])
             for w in range(4):
                 nc.sync.dma_start(words[g][w][:], toks[w][:, columns])
+            if g == 0:
+                nc.sync.dma_start(offsets[:], offs)
             for h in range(g * GROUP, (g + 1) * GROUP):
                 memory.append(held.tile([P, S], F32, name=f"memory{h}"))
                 nc.sync.dma_start(memory[h][:], base_blocks[h])

@@ -15,9 +15,9 @@ GROUPS = BLOCKS // GROUP
 
 def tile_decoderrkbmemnn_s_kernel(tc, base, tok0, tok1, tok2, tok3, offs, out):
     nc = tc.nc
-    toks = [tok.rearrange("(p h) n -> p (h n)", h=BLOCKS) for tok in (tok0, tok1, tok2, tok3)]
-    base_blocks = base.rearrange("(p h) s -> h p s", h=BLOCKS)
-    out_blocks = out.rearrange("(p h) s -> h p s", h=BLOCKS)
+    toks = [tok.rearrange("(g p i) n -> g p (i n)", p=P, i=GROUP) for tok in (tok0, tok1, tok2, tok3)]
+    base_groups = base.rearrange("(g p i) s -> g i p s", p=P, i=GROUP)
+    out_groups = out.rearrange("(g p i) s -> g i p s", p=P, i=GROUP)
 
     with tc.tile_pool(name="held", bufs=1) as held:
         offsets = held.tile([P, N // 16], U16, name="offsets")
@@ -25,15 +25,14 @@ def tile_decoderrkbmemnn_s_kernel(tc, base, tok0, tok1, tok2, tok3, offs, out):
         words = []
         memory = []
         for g in range(GROUPS):
-            columns = slice(g * GROUP * N, (g + 1) * GROUP * N)
             words.append([held.tile([P, GROUP * N], F32, name=f"word{w}_{g}") for w in range(4)])
             for w in range(4):
-                nc.sync.dma_start(words[g][w][:], toks[w][:, columns])
+                nc.sync.dma_start(words[g][w][:], toks[w][g])
             if g == 0:
                 nc.sync.dma_start(offsets[:], offs)
             for h in range(g * GROUP, (g + 1) * GROUP):
                 memory.append(held.tile([P, S], F32, name=f"memory{h}"))
-                nc.sync.dma_start(memory[h][:], base_blocks[h])
+                nc.sync.dma_start(memory[h][:], base_groups[g][h % GROUP])
 
         for g in range(GROUPS):
             pair01 = held.tile([P, GROUP * N], F32, name=f"pair01_{g}")
@@ -47,4 +46,4 @@ def tile_decoderrkbmemnn_s_kernel(tc, base, tok0, tok1, tok2, tok3, offs, out):
                 )
 
         for h in range(BLOCKS):
-            nc.sync.dma_start(out_blocks[h], memory[h][:])
+            nc.sync.dma_start(out_groups[h // GROUP][h % GROUP], memory[h][:])

@@ -15,35 +15,40 @@ GROUPS = BLOCKS // GROUP
 
 def tile_decoderrkbmemnn_s_kernel(tc, base, tok0, tok1, tok2, tok3, offs, out):
     nc = tc.nc
-    toks = [tok.rearrange("(g p i) n -> g p (i n)", p=P, i=GROUP) for tok in (tok0, tok1, tok2, tok3)]
-    base_groups = base.rearrange("(g p i) s -> g i p s", p=P, i=GROUP)
-    out_groups = out.rearrange("(g p i) s -> g i p s", p=P, i=GROUP)
+    whole = [tok.rearrange("(p h) n -> p (h n)", h=BLOCKS) for tok in (tok0, tok1, tok2)]
+    last = tok3.rearrange("(p g i) n -> g p (i n)", g=GROUPS, i=GROUP)
+    base_blocks = base.rearrange("(p h) s -> h p s", h=BLOCKS)
+    out_blocks = out.rearrange("(p h) s -> h p s", h=BLOCKS)
 
     with tc.tile_pool(name="held", bufs=1) as held:
         offsets = held.tile([P, N // 16], U16, name="offsets")
 
-        words = []
+        words = [held.tile([P, BLOCKS * N], F32, name=f"word{w}") for w in range(3)]
+        for w in range(3):
+            nc.sync.dma_start(words[w][:], whole[w])
+        last_words = []
         memory = []
         for g in range(GROUPS):
-            words.append([held.tile([P, GROUP * N], F32, name=f"word{w}_{g}") for w in range(4)])
-            for w in range(4):
-                nc.sync.dma_start(words[g][w][:], toks[w][g])
+            last_words.append(held.tile([P, GROUP * N], F32, name=f"last_word_{g}"))
+            nc.sync.dma_start(last_words[g][:], last[g])
             if g == 0:
                 nc.sync.dma_start(offsets[:], offs)
             for h in range(g * GROUP, (g + 1) * GROUP):
                 memory.append(held.tile([P, S], F32, name=f"memory{h}"))
-                nc.sync.dma_start(memory[h][:], base_groups[g][h % GROUP])
+                nc.sync.dma_start(memory[h][:], base_blocks[h])
 
-        for g in range(GROUPS):
-            pair01 = held.tile([P, GROUP * N], F32, name=f"pair01_{g}")
-            pair23 = held.tile([P, GROUP * N], F32, name=f"pair23_{g}")
-            nc.vector.tensor_tensor(pair01[:], words[g][0][:], words[g][1][:], ADD)
-            nc.vector.tensor_tensor(pair23[:], words[g][2][:], words[g][3][:], ADD)
-            for i in range(GROUP):
-                entries = slice(i * N, (i + 1) * N)
-                nc.vector.tensor_tensor(
-                    memory[g * GROUP + i][:].indirect(offsets[:]), pair01[:, entries], pair23[:, entries], ADD
-                )
+        sum01 = held.tile([P, BLOCKS * N], F32, name="sum01")
+        sum012 = held.tile([P, BLOCKS * N], F32, name="sum012")
+        nc.vector.tensor_tensor(sum01[:], words[0][:], words[1][:], ADD)
+        nc.vector.tensor_tensor(sum012[:], sum01[:], words[2][:], ADD)
+        for h in range(BLOCKS):
+            g, i = divmod(h, GROUP)
+            nc.vector.tensor_tensor(
+                memory[h][:].indirect(offsets[:]),
+                sum012[:, h * N : (h + 1) * N],
+                last_words[g][:, i * N : (i + 1) * N],
+                ADD,
+            )
 
         for h in range(BLOCKS):
-            nc.sync.dma_start(out_groups[h // GROUP][h % GROUP], memory[h][:])
+            nc.sync.dma_start(out_blocks[h], memory[h][:])

@@ -9,14 +9,12 @@ ADD = mybir.AluOpType.add
 
 BYTES = 4 * (C * S + 4 * C * N + C * (S - N)) + 2 * P * (N // 16)
 
-GROUP = 2
-GROUPS = BLOCKS // GROUP
+PARTS = [(0, 1), (1, 2), (2, 4)]
 
 
 def tile_decoderrkbmemnn_s_kernel(tc, base, tok0, tok1, tok2, tok3, offs, out):
     nc = tc.nc
-    whole = [tok.rearrange("(p h) n -> p (h n)", h=BLOCKS) for tok in (tok0, tok1, tok2)]
-    last = tok3.rearrange("(p g i) n -> g p (i n)", g=GROUPS, i=GROUP)
+    whole = [tok.rearrange("(p h) n -> p (h n)", h=BLOCKS) for tok in (tok0, tok1, tok2, tok3)]
     base_blocks = base.rearrange("(p h) s -> h p s", h=BLOCKS)
     out_blocks = out.rearrange("(p h) s -> h p s", h=BLOCKS)
 
@@ -28,12 +26,13 @@ def tile_decoderrkbmemnn_s_kernel(tc, base, tok0, tok1, tok2, tok3, offs, out):
             nc.sync.dma_start(words[w][:], whole[w])
         last_words = []
         memory = []
-        for g in range(GROUPS):
-            last_words.append(held.tile([P, GROUP * N], F32, name=f"last_word_{g}"))
-            nc.sync.dma_start(last_words[g][:], last[g])
-            if g == 0:
+        for first, end in PARTS:
+            part = held.tile([P, (end - first) * N], F32, name=f"last_word_from{first}")
+            nc.sync.dma_start(part[:], whole[3][:, first * N : end * N])
+            if first == 0:
                 nc.sync.dma_start(offsets[:], offs)
-            for h in range(g * GROUP, (g + 1) * GROUP):
+            for h in range(first, end):
+                last_words.append(part[:, (h - first) * N : (h - first + 1) * N])
                 memory.append(held.tile([P, S], F32, name=f"memory{h}"))
                 nc.sync.dma_start(memory[h][:], base_blocks[h])
 
@@ -42,12 +41,8 @@ def tile_decoderrkbmemnn_s_kernel(tc, base, tok0, tok1, tok2, tok3, offs, out):
         nc.vector.tensor_tensor(sum01[:], words[0][:], words[1][:], ADD)
         nc.vector.tensor_tensor(sum012[:], sum01[:], words[2][:], ADD)
         for h in range(BLOCKS):
-            g, i = divmod(h, GROUP)
             nc.vector.tensor_tensor(
-                memory[h][:].indirect(offsets[:]),
-                sum012[:, h * N : (h + 1) * N],
-                last_words[g][:, i * N : (i + 1) * N],
-                ADD,
+                memory[h][:].indirect(offsets[:]), sum012[:, h * N : (h + 1) * N], last_words[h], ADD
             )
 
         for h in range(BLOCKS):

@@ -46,4 +46,5 @@ def tile_decoderrkbmemnn_s_kernel(tc, base, tok0, tok1, tok2, tok3, offs, out):
             )
 
         for h in range(BLOCKS):
-            nc.sync.dma_start(out_blocks[h], memory[h][:])
+            queue = nc.sync if h % 2 == 0 else nc.scalar
+            queue.dma_start(out_blocks[h], memory[h][:])

@@ -11,6 +11,8 @@ BYTES = 4 * (C * S + 4 * C * N + C * (S - N)) + 2 * P * (N // 16)
 
 PARTS = [(0, 1), (1, 2), (2, 4)]
 
+LINE = 256
+
 
 def tile_decoderrkbmemnn_s_kernel(tc, base, tok0, tok1, tok2, tok3, offs, out):
     nc = tc.nc
@@ -21,19 +23,19 @@ def tile_decoderrkbmemnn_s_kernel(tc, base, tok0, tok1, tok2, tok3, offs, out):
     with tc.tile_pool(name="held", bufs=1) as held:
         offsets = held.tile([P, N // 16], U16, name="offsets")
 
-        words = [held.tile([P, BLOCKS * N], F32, name=f"word{w}") for w in range(3)]
+        words = [held.tile([P, BLOCKS * N], F32, name=f"word{w}", align_bytes=LINE) for w in range(3)]
         for w in range(3):
             nc.sync.dma_start(words[w][:], whole[w])
         last_words = []
         memory = []
         for first, end in PARTS:
-            part = held.tile([P, (end - first) * N], F32, name=f"last_word_from{first}")
+            part = held.tile([P, (end - first) * N], F32, name=f"last_word_from{first}", align_bytes=LINE)
             nc.sync.dma_start(part[:], whole[3][:, first * N : end * N])
             if first == 0:
                 nc.sync.dma_start(offsets[:], offs)
             for h in range(first, end):
                 last_words.append(part[:, (h - first) * N : (h - first + 1) * N])
-                memory.append(held.tile([P, S], F32, name=f"memory{h}"))
+                memory.append(held.tile([P, S], F32, name=f"memory{h}", align_bytes=LINE))
                 nc.sync.dma_start(memory[h][:], base_blocks[h])
 
         sum01 = held.tile([P, BLOCKS * N], F32, name="sum01")

@@ -1,4 +1,5 @@
 import concourse.mybir as mybir
+from concourse.masks import make_identity
 
 P = 128
 C, S, N = 512, 2048, 512
@@ -9,7 +10,7 @@ ADD = mybir.AluOpType.add
 
 BYTES = 4 * (C * S + 4 * C * N + C * (S - N)) + 2 * P * (N // 16)
 
-PARTS = [(0, 1), (1, 2), (2, 4)]
+GROUP = 2
 
 LINE = 256
 
@@ -20,33 +21,40 @@ def tile_decoderrkbmemnn_s_kernel(tc, base, tok0, tok1, tok2, tok3, offs, out):
     base_blocks = base.rearrange("(p h) s -> h p s", h=BLOCKS)
     out_blocks = out.rearrange("(p h) s -> h p s", h=BLOCKS)
 
-    with tc.tile_pool(name="held", bufs=1) as held:
+    with tc.tile_pool(name="held", bufs=1) as held, tc.psum_pool(name="psum", bufs=BLOCKS - GROUP) as psum:
         offsets = held.tile([P, N // 16], U16, name="offsets")
 
-        words = [held.tile([P, BLOCKS * N], F32, name=f"word{w}", align_bytes=LINE) for w in range(3)]
-        for w in range(3):
-            nc.sync.dma_start(words[w][:], whole[w])
-        last_words = []
-        memory = []
-        for first, end in PARTS:
-            part = held.tile([P, (end - first) * N], F32, name=f"last_word_from{first}", align_bytes=LINE)
-            nc.sync.dma_start(part[:], whole[3][:, first * N : end * N])
+        words = [held.tile([P, BLOCKS * N], F32, name=f"word{w}", align_bytes=LINE) for w in range(4)]
+        memory = [held.tile([P, S], F32, name=f"memory{h}", align_bytes=LINE) for h in range(BLOCKS)]
+        nc.sync.dma_start(words[0][:], whole[0])
+        nc.sync.dma_start(words[1][:], whole[1])
+        for first in range(0, BLOCKS, GROUP):
+            columns = slice(first * N, (first + GROUP) * N)
+            nc.sync.dma_start(words[2][:, columns], whole[2][:, columns])
+            nc.sync.dma_start(words[3][:, columns], whole[3][:, columns])
             if first == 0:
                 nc.sync.dma_start(offsets[:], offs)
-            for h in range(first, end):
-                last_words.append(part[:, (h - first) * N : (h - first + 1) * N])
-                memory.append(held.tile([P, S], F32, name=f"memory{h}", align_bytes=LINE))
+            for h in range(first, first + GROUP):
                 nc.sync.dma_start(memory[h][:], base_blocks[h])
 
+        identity = held.tile([P, P], F32, name="identity")
+        make_identity(nc, identity[:])
         sum01 = held.tile([P, BLOCKS * N], F32, name="sum01")
         sum012 = held.tile([P, BLOCKS * N], F32, name="sum012")
         nc.vector.tensor_tensor(sum01[:], words[0][:], words[1][:], ADD)
-        nc.vector.tensor_tensor(sum012[:], sum01[:], words[2][:], ADD)
+        early = slice(0, GROUP * N)
+        nc.vector.tensor_tensor(sum012[:, early], sum01[:, early], words[2][:, early], ADD)
+        for h in range(GROUP, BLOCKS):
+            entries = slice(h * N, (h + 1) * N)
+            total = psum.tile([P, N], F32, name="total")
+            nc.tensor.matmul(total[:], identity[:], sum01[:, entries], start=True, stop=False)
+            nc.tensor.matmul(total[:], identity[:], words[2][:, entries], start=False, stop=True)
+            nc.scalar.copy(sum012[:, entries], total[:])
         for h in range(BLOCKS):
+            entries = slice(h * N, (h + 1) * N)
             nc.vector.tensor_tensor(
-                memory[h][:].indirect(offsets[:]), sum012[:, h * N : (h + 1) * N], last_words[h], ADD
+                memory[h][:].indirect(offsets[:]), sum012[:, entries], words[3][:, entries], ADD
             )
 
         for h in range(BLOCKS):
-            queue = nc.sync if h % 2 == 0 else nc.scalar
-            queue.dma_start(out_blocks[h], memory[h][:])
+            nc.sync.dma_start(out_blocks[h], memory[h][:])

import concourse.mybir as mybir
from concourse.masks import make_identity

P = 128
C, S, N = 512, 2048, 512
BLOCKS = C // P
F32 = mybir.dt.float32
U16 = mybir.dt.uint16
ADD = mybir.AluOpType.add

BYTES = 4 * (C * S + 4 * C * N + C * (S - N)) + 2 * P * (N // 16)

GROUP = 2

LINE = 256


def tile_decoderrkbmemnn_s_kernel(tc, base, tok0, tok1, tok2, tok3, offs, out):
    nc = tc.nc
    whole = [tok.rearrange("(p h) n -> p (h n)", h=BLOCKS) for tok in (tok0, tok1, tok2, tok3)]
    base_blocks = base.rearrange("(p h) s -> h p s", h=BLOCKS)
    out_blocks = out.rearrange("(p h) s -> h p s", h=BLOCKS)

    with tc.tile_pool(name="held", bufs=1) as held, tc.psum_pool(name="psum", bufs=BLOCKS - GROUP) as psum:
        offsets = held.tile([P, N // 16], U16, name="offsets")

        words = [held.tile([P, BLOCKS * N], F32, name=f"word{w}", align_bytes=LINE) for w in range(4)]
        memory = [held.tile([P, S], F32, name=f"memory{h}", align_bytes=LINE) for h in range(BLOCKS)]
        nc.sync.dma_start(words[0][:], whole[0])
        nc.sync.dma_start(words[1][:], whole[1])
        for first in range(0, BLOCKS, GROUP):
            columns = slice(first * N, (first + GROUP) * N)
            nc.sync.dma_start(words[2][:, columns], whole[2][:, columns])
            nc.sync.dma_start(words[3][:, columns], whole[3][:, columns])
            if first == 0:
                nc.sync.dma_start(offsets[:], offs)
            for h in range(first, first + GROUP):
                nc.sync.dma_start(memory[h][:], base_blocks[h])

        identity = held.tile([P, P], F32, name="identity")
        make_identity(nc, identity[:])
        sum01 = held.tile([P, BLOCKS * N], F32, name="sum01")
        sum012 = held.tile([P, BLOCKS * N], F32, name="sum012")
        nc.vector.tensor_tensor(sum01[:], words[0][:], words[1][:], ADD)
        early = slice(0, GROUP * N)
        nc.vector.tensor_tensor(sum012[:, early], sum01[:, early], words[2][:, early], ADD)
        for h in range(GROUP, BLOCKS):
            entries = slice(h * N, (h + 1) * N)
            total = psum.tile([P, N], F32, name="total")
            nc.tensor.matmul(total[:], identity[:], sum01[:, entries], start=True, stop=False)
            nc.tensor.matmul(total[:], identity[:], words[2][:, entries], start=False, stop=True)
            nc.scalar.copy(sum012[:, entries], total[:])
        for h in range(BLOCKS):
            entries = slice(h * N, (h + 1) * N)
            nc.vector.tensor_tensor(
                memory[h][:].indirect(offsets[:]), sum012[:, entries], words[3][:, entries], ADD
            )

        for h in range(BLOCKS):
            nc.sync.dma_start(out_blocks[h], memory[h][:])
